import numpy as np
import ml_dtypes


def mxq(x, axis, fmt="e4m3"):
    dtype, down = {"e4m3": (ml_dtypes.float8_e4m3fn, 7), "e5m2": (ml_dtypes.float8_e5m2, 14)}[fmt]
    v = np.moveaxis(np.asarray(x, np.float32).astype(ml_dtypes.bfloat16).astype(np.float64), axis, -1)
    blocks = v.reshape(v.shape[:-1] + (-1, 32))
    amax = np.abs(blocks).max(-1, keepdims=True)
    byte = np.maximum(np.where(amax > 0, np.frexp(amax)[1] - 1 + 127, 0) - down, 1)
    scale = np.exp2(byte - 127.0)
    codes = (blocks / scale).astype(np.float32).astype(dtype).astype(np.float64)
    return np.moveaxis((codes * scale).reshape(v.shape), -1, axis)


WIDE = False


def mx_kscale(k):
    if not WIDE:
        return np.ones(k)
    levels = np.array([10, -10, 5, -5, 0])
    a = np.random.permutation(np.resize(levels, k // 512 * 4)).reshape(k // 512, 4)
    idx = np.arange(k)
    return np.exp2(a[idx // 512, idx % 128 // 32])


BF16 = ml_dtypes.bfloat16


def bf(x):
    return np.asarray(x, np.float32).astype(BF16)


def f64(x):
    return np.asarray(x).astype(np.float64)


N, C, O, OH, OW, KH, KW, STRIDE, PAD = 512, 512, 256, 3, 3, 3, 3, 1, 1
H, W = (OH - 1) * STRIDE + KH - 2 * PAD, (OW - 1) * STRIDE + KW - 2 * PAD
NEG_SLOPE = 0.1


def span(t, n_out, n_in):
    ok = [p for p in range(n_out) if 0 <= p * STRIDE + t - PAD < n_in]
    return ok[0], ok[-1] + 1


def setup_inputs():
    s = mx_kscale(C)
    return {"x": bf(np.random.standard_normal((N, C, H, W)) * s[None, :, None, None]),
            "weight": bf(np.random.standard_normal((1, O, C, OH, OW, KH * KW)) * np.sqrt(2.0 / (KH * KW * C)) / s[None, None, :, None, None, None]),
            "bias": bf(np.random.standard_normal((1, O, OH, OW)) * 0.3)}


def reference(x, weight, bias):
    xq = mxq(f64(x), 1, "e4m3")
    wt = f64(weight)[0]
    acc = np.zeros((N, O, OH, OW))
    for i in range(KH):
        h0, h1 = span(i, OH, H)
        a0 = h0 * STRIDE + i - PAD
        for j in range(KW):
            w0, w1 = span(j, OW, W)
            b0 = w0 * STRIDE + j - PAD
            xs = xq[:, :, a0:a0 + (h1 - h0 - 1) * STRIDE + 1:STRIDE, b0:b0 + (w1 - w0 - 1) * STRIDE + 1:STRIDE]
            wq = mxq(wt[:, :, h0:h1, w0:w1, i * KW + j], 1, "e4m3")
            p = xs.transpose(2, 3, 0, 1) @ wq.transpose(2, 3, 1, 0)
            acc[:, :, h0:h1, w0:w1] += p.transpose(2, 3, 0, 1)
    out = acc + f64(bias)
    return np.where(out >= 0, out, NEG_SLOPE * out)

@@ -1,0 +1,161 @@
+import concourse.mybir as mybir
+from concourse.masks import make_identity
+
+BF16 = mybir.dt.bfloat16
+F32 = mybir.dt.float32
+U32 = mybir.dt.uint32
+U8 = mybir.dt.uint8
+FP8X4 = mybir.dt.float8_e4m3fn_x4
+ALU = mybir.AluOpType
+
+P = 128
+PACK = 4
+N, C, O = 512, 512, 256
+SIDE = 3
+PLACES = SIDE * SIDE
+TAPS = SIDE * SIDE
+PAD = 1
+NEG_SLOPE = 0.1
+
+N_TILES = N // P
+O_BLOCK = 128
+O_BLOCKS = O // O_BLOCK
+O_CHUNK = 32
+MAX_TAPS_PER_QUANTISE = 8
+
+USED_TAPS = 49
+FLOPS = 2 * N * C * O * USED_TAPS
+BYTES = 2 * N * C * PLACES + 2 * O * C * USED_TAPS + 2 * O * PLACES + 4 * N * O * PLACES
+
+
+def taps_inside(coordinate):
+    return range(max(0, PAD - coordinate), min(SIDE, SIDE + PAD - coordinate))
+
+
+def tile_locallyconnected2d_t_kernel(tc, x, weight, bias, out):
+    nc = tc.nc
+
+    x_rows = x.rearrange("n c h w -> n c (h w)")
+    w_rows = weight.rearrange("a o (p t) h w k -> p (a o) t (h w k)", t=PACK)
+    bias_row = bias.rearrange("a o h w -> (a o h w)")
+    out_rows = out.rearrange("n o h w -> n o (h w)")
+
+    with tc.tile_pool(name="keep", bufs=1) as keep, tc.tile_pool(name="w_load", bufs=3) as w_load, tc.tile_pool(
+        name="w_group", bufs=1
+    ) as w_group, tc.psum_pool(name="psum_x", bufs=3) as psum_x, tc.psum_pool(name="psum_acc", bufs=4) as psum_acc:
+        identity = keep.tile([P, P], F32)
+        make_identity(nc, identity[:])
+
+        bias_raw = keep.tile([P, O, PLACES], BF16)
+        nc.gpsimd.dma_start(out=bias_raw[:].rearrange("p o s -> p (o s)"), in_=bias_row.partition_broadcast(P))
+        bias_all = keep.tile([P, PLACES, O], F32)
+        nc.vector.tensor_copy(out=bias_all[:], in_=bias_raw[:].rearrange("p o s -> p s o"))
+
+        x_codes = keep.tile([P, N_TILES, PLACES, P], U32, align_bytes=64)
+        x_scales = keep.tile([P, N_TILES, PLACES, P], U8, align_bytes=64)
+        with tc.tile_pool(name="x_stage", bufs=2) as x_stage:
+            for nt in range(N_TILES):
+                x_raw = x_stage.tile([P, C, PLACES], BF16)
+                nc.sync.dma_start(out=x_raw[:], in_=x_rows[nt * P : (nt + 1) * P])
+
+                x_sorted = x_stage.tile([P, PLACES, C], BF16)
+                for row in range(SIDE):
+                    places = slice(row * SIDE, (row + 1) * SIDE)
+                    copy = nc.scalar.copy if row == SIDE - 1 else nc.vector.tensor_copy
+                    copy(out=x_sorted[:, places, :].rearrange("p s c -> p c s"), in_=x_raw[:, :, places])
+
+                x_grouped = x_stage.tile([P, PLACES, P, 2], F32, align_bytes=64)
+                for s in range(PLACES):
+                    words = x_sorted[:, s, :].bitcast(F32).rearrange("p (q u) -> p u q", u=2)
+                    x_t = psum_x.tile([P, 2, P], F32)
+                    for u in range(2):
+                        nc.tensor.transpose(x_t[:, u, :], words[:, u, :], identity[:])
+                    copy = nc.scalar.copy if s % 2 == 1 else nc.vector.tensor_copy
+                    copy(out=x_grouped[:, s, :, :], in_=x_t[:].rearrange("p u n -> p n u"))
+
+                first = 0
+                while first < PLACES:
+                    count = min(MAX_TAPS_PER_QUANTISE, PLACES - first)
+                    nc.vector.quantize_mx(
+                        out=x_codes[:, nt, first : first + count, :].rearrange("p s n -> p (s n)").bitcast(FP8X4),
+                        scales=x_scales[:, nt, first : first + count, :].rearrange("p s n -> p (s n)"),
+                        in_=x_grouped[:, first : first + count, :, :].rearrange("p s n u -> p (s n u)").bitcast(BF16),
+                    )
+                    first += count
+
+        with tc.tile_pool(name="w_words", bufs=1) as w_words, tc.tile_pool(name="result", bufs=2) as result:
+            for block in range(O_BLOCKS):
+                w_grouped = []
+                for place in range(PLACES):
+                    n_taps = len(taps_inside(place // SIDE)) * len(taps_inside(place % SIDE))
+                    w_grouped.append(
+                        w_group.tile([P, n_taps, O_BLOCK, PACK], BF16, name="w_grouped%d" % place, align_bytes=64)
+                    )
+
+                for chunk in range(O_BLOCK // O_CHUNK):
+                    first_o = block * O_BLOCK + chunk * O_CHUNK
+                    w_raw = w_load.tile([P, O_CHUNK, PACK, PLACES * TAPS], BF16)
+                    nc.sync.dma_start(out=w_raw[:], in_=w_rows[:, first_o : first_o + O_CHUNK])
+                    for place in range(PLACES):
+                        h, w = place // SIDE, place % SIDE
+                        copy = nc.vector.tensor_copy if h == 1 else nc.scalar.copy
+                        cols = taps_inside(w)
+                        for r, i in enumerate(taps_inside(h)):
+                            f = place * TAPS + i * SIDE + cols[0]
+                            slot = r * len(cols)
+                            copy(
+                                out=w_grouped[place][
+                                    :, slot : slot + len(cols), chunk * O_CHUNK : (chunk + 1) * O_CHUNK, :
+                                ].rearrange("p j o t -> p o j t"),
+                                in_=w_raw[:, :, :, f : f + len(cols)].rearrange("p o t j -> p o j t"),
+                            )
+
+                w_codes = []
+                w_scales = []
+                for place in range(PLACES):
+                    n_taps = w_grouped[place].shape[1]
+                    codes = w_words.tile([P, n_taps, O_BLOCK], U32, name="w_codes%d" % place, align_bytes=64)
+                    scales = w_words.tile([P, n_taps, O_BLOCK], U8, name="w_scales%d" % place, align_bytes=64)
+                    first = 0
+                    while first < n_taps:
+                        count = MAX_TAPS_PER_QUANTISE
+                        while count > n_taps - first:
+                            count //= 2
+                        nc.vector.quantize_mx(
+                            out=codes[:, first : first + count, :].rearrange("p j o -> p (j o)").bitcast(FP8X4),
+                            scales=scales[:, first : first + count, :].rearrange("p j o -> p (j o)"),
+                            in_=w_grouped[place][:, first : first + count, :, :].rearrange("p j o t -> p (j o t)"),
+                        )
+                        first += count
+                    w_codes.append(codes)
+                    w_scales.append(scales)
+
+                o_cols = slice(block * O_BLOCK, (block + 1) * O_BLOCK)
+                for nt in range(N_TILES):
+                    biased = result.tile([P, PLACES, O_BLOCK], F32)
+                    for h in range(SIDE):
+                        acc = psum_acc.tile([P, SIDE, O_BLOCK], F32)
+                        for w in range(SIDE):
+                            place = h * SIDE + w
+                            taps = [(i, j) for i in taps_inside(h) for j in taps_inside(w)]
+                            for slot, (i, j) in enumerate(taps):
+                                x_place = (h + i - PAD) * SIDE + (w + j - PAD)
+                                nc.tensor.matmul_mx(
+                                    out=acc[:, w, :],
+                                    lhsT=x_codes[:, nt, x_place, :].bitcast(FP8X4),
+                                    lhsT_scale=x_scales[:, nt, x_place, :],
+                                    rhs=w_codes[place][:, slot, :].bitcast(FP8X4),
+                                    rhs_scale=w_scales[place][:, slot, :],
+                                    start=(slot == 0),
+                                    stop=(slot == len(taps) - 1),
+                                )
+                        places = slice(h * SIDE, (h + 1) * SIDE)
+                        nc.vector.tensor_tensor(
+                            out=biased[:, places, :], in0=acc[:], in1=bias_all[:, places, o_cols], op=ALU.add
+                        )
+                    by_channel = biased[:].rearrange("p s o -> p o s")
+                    final = result.tile([P, O_BLOCK, PLACES], F32)
+                    nc.vector.scalar_tensor_tensor(
+                        out=final[:], in0=by_channel, scalar=NEG_SLOPE, in1=by_channel, op0=ALU.mult, op1=ALU.max
+                    )
+                    nc.gpsimd.dma_start(out=out_rows[nt * P : (nt + 1) * P, o_cols], in_=final[:])

@@ -20,7 +20,9 @@ NEG_SLOPE = 0.1
 N_TILES = N // P
 O_BLOCK = 128
 O_BLOCKS = O // O_BLOCK
-O_CHUNK = 32
+O_CHUNK = 16
+CHUNKS = O_BLOCK // O_CHUNK
+W_BUFFERS = 6
 MAX_TAPS_PER_QUANTISE = 8
 
 USED_TAPS = 49
@@ -40,33 +42,51 @@ def tile_locallyconnected2d_t_kernel(tc, x, weight, bias, out):
     bias_row = bias.rearrange("a o h w -> (a o h w)")
     out_rows = out.rearrange("n o h w -> n o (h w)")
 
-    with tc.tile_pool(name="keep", bufs=1) as keep, tc.tile_pool(name="w_load", bufs=3) as w_load, tc.tile_pool(
-        name="w_group", bufs=1
-    ) as w_group, tc.psum_pool(name="psum_x", bufs=3) as psum_x, tc.psum_pool(name="psum_acc", bufs=4) as psum_acc:
+    with tc.manual_schedule(), tc.tile_pool(name="keep", bufs=1) as keep, tc.tile_pool(
+        name="w_load", bufs=W_BUFFERS
+    ) as w_load, tc.tile_pool(name="w_group", bufs=1) as w_group, tc.psum_pool(
+        name="psum_x", bufs=3
+    ) as psum_x, tc.psum_pool(name="psum_acc", bufs=4) as psum_acc:
         identity = keep.tile([P, P], F32)
         make_identity(nc, identity[:])
 
         bias_raw = keep.tile([P, O, PLACES], BF16)
         nc.gpsimd.dma_start(out=bias_raw[:].rearrange("p o s -> p (o s)"), in_=bias_row.partition_broadcast(P))
         bias_all = keep.tile([P, PLACES, O], F32)
-        nc.vector.tensor_copy(out=bias_all[:], in_=bias_raw[:].rearrange("p o s -> p s o"))
+        nc.gpsimd.tensor_copy(out=bias_all[:], in_=bias_raw[:].rearrange("p o s -> p s o"))
+
+        w_raw = []
+
+        def load_weights(k):
+            w_raw.append(w_load.tile([P, O_CHUNK, PACK, PLACES * TAPS], BF16, name="w_raw", tag="w_raw"))
+            nc.sync.dma_start(out=w_raw[k][:], in_=w_rows[:, k * O_CHUNK : (k + 1) * O_CHUNK])
 
         x_codes = keep.tile([P, N_TILES, PLACES, P], U32, align_bytes=64)
         x_scales = keep.tile([P, N_TILES, PLACES, P], U8, align_bytes=64)
-        with tc.tile_pool(name="x_stage", bufs=2) as x_stage:
+        with tc.tile_pool(name="x_load", bufs=N_TILES) as x_load, tc.tile_pool(name="x_stage", bufs=2) as x_stage:
+            x_raw = []
             for nt in range(N_TILES):
-                x_raw = x_stage.tile([P, C, PLACES], BF16)
-                nc.sync.dma_start(out=x_raw[:], in_=x_rows[nt * P : (nt + 1) * P])
+                x_raw.append(x_load.tile([P, C, PLACES], BF16, name="x_raw", tag="x_raw"))
+                nc.sync.dma_start(out=x_raw[nt][:], in_=x_rows[nt * P : (nt + 1) * P])
+            for k in range(W_BUFFERS - 1):
+                load_weights(k)
 
-                x_sorted = x_stage.tile([P, PLACES, C], BF16)
+            x_sorted = []
+
+            def sort_by_place(nt):
+                x_sorted.append(x_stage.tile([P, PLACES, C], BF16, name="x_sorted", tag="x_sorted"))
                 for row in range(SIDE):
                     places = slice(row * SIDE, (row + 1) * SIDE)
                     copy = nc.scalar.copy if row == SIDE - 1 else nc.vector.tensor_copy
-                    copy(out=x_sorted[:, places, :].rearrange("p s c -> p c s"), in_=x_raw[:, :, places])
+                    copy(out=x_sorted[nt][:, places, :].rearrange("p s c -> p c s"), in_=x_raw[nt][:, :, places])
 
+            sort_by_place(0)
+            for nt in range(N_TILES):
+                if nt + 1 < N_TILES:
+                    sort_by_place(nt + 1)
                 x_grouped = x_stage.tile([P, PLACES, P, 2], F32, align_bytes=64)
                 for s in range(PLACES):
-                    words = x_sorted[:, s, :].bitcast(F32).rearrange("p (q u) -> p u q", u=2)
+                    words = x_sorted[nt][:, s, :].bitcast(F32).rearrange("p (q u) -> p u q", u=2)
                     x_t = psum_x.tile([P, 2, P], F32)
                     for u in range(2):
                         nc.tensor.transpose(x_t[:, u, :], words[:, u, :], identity[:])
@@ -83,33 +103,25 @@ def tile_locallyconnected2d_t_kernel(tc, x, weight, bias, out):
                     )
                     first += count
 
-        with tc.tile_pool(name="w_words", bufs=1) as w_words, tc.tile_pool(name="result", bufs=2) as result:
-            for block in range(O_BLOCKS):
-                w_grouped = []
+        with tc.tile_pool(name="w_words", bufs=1) as w_words, tc.tile_pool(
+            name="sums", bufs=2
+        ) as sums, tc.tile_pool(name="result", bufs=N_TILES) as result:
+
+            def regroup(k, w_grouped):
+                o_cols = slice((k % CHUNKS) * O_CHUNK, (k % CHUNKS + 1) * O_CHUNK)
                 for place in range(PLACES):
-                    n_taps = len(taps_inside(place // SIDE)) * len(taps_inside(place % SIDE))
-                    w_grouped.append(
-                        w_group.tile([P, n_taps, O_BLOCK, PACK], BF16, name="w_grouped%d" % place, align_bytes=64)
-                    )
+                    h, w = place // SIDE, place % SIDE
+                    copy = nc.vector.tensor_copy if h == 1 else nc.scalar.copy
+                    cols = taps_inside(w)
+                    for r, i in enumerate(taps_inside(h)):
+                        f = place * TAPS + i * SIDE + cols[0]
+                        slot = r * len(cols)
+                        copy(
+                            out=w_grouped[place][:, slot : slot + len(cols), o_cols, :].rearrange("p j o t -> p o j t"),
+                            in_=w_raw[k][:, :, :, f : f + len(cols)].rearrange("p o t j -> p o j t"),
+                        )
 
-                for chunk in range(O_BLOCK // O_CHUNK):
-                    first_o = block * O_BLOCK + chunk * O_CHUNK
-                    w_raw = w_load.tile([P, O_CHUNK, PACK, PLACES * TAPS], BF16)
-                    nc.sync.dma_start(out=w_raw[:], in_=w_rows[:, first_o : first_o + O_CHUNK])
-                    for place in range(PLACES):
-                        h, w = place // SIDE, place % SIDE
-                        copy = nc.vector.tensor_copy if h == 1 else nc.scalar.copy
-                        cols = taps_inside(w)
-                        for r, i in enumerate(taps_inside(h)):
-                            f = place * TAPS + i * SIDE + cols[0]
-                            slot = r * len(cols)
-                            copy(
-                                out=w_grouped[place][
-                                    :, slot : slot + len(cols), chunk * O_CHUNK : (chunk + 1) * O_CHUNK, :
-                                ].rearrange("p j o t -> p o j t"),
-                                in_=w_raw[:, :, :, f : f + len(cols)].rearrange("p o t j -> p o j t"),
-                            )
-
+            def quantise(w_grouped):
                 w_codes = []
                 w_scales = []
                 for place in range(PLACES):
@@ -129,33 +141,61 @@ def tile_locallyconnected2d_t_kernel(tc, x, weight, bias, out):
                         first += count
                     w_codes.append(codes)
                     w_scales.append(scales)
+                return w_codes, w_scales
 
+            def products(block, nt, w_codes, w_scales):
                 o_cols = slice(block * O_BLOCK, (block + 1) * O_BLOCK)
-                for nt in range(N_TILES):
-                    biased = result.tile([P, PLACES, O_BLOCK], F32)
-                    for h in range(SIDE):
-                        acc = psum_acc.tile([P, SIDE, O_BLOCK], F32)
-                        for w in range(SIDE):
-                            place = h * SIDE + w
-                            taps = [(i, j) for i in taps_inside(h) for j in taps_inside(w)]
-                            for slot, (i, j) in enumerate(taps):
-                                x_place = (h + i - PAD) * SIDE + (w + j - PAD)
-                                nc.tensor.matmul_mx(
-                                    out=acc[:, w, :],
-                                    lhsT=x_codes[:, nt, x_place, :].bitcast(FP8X4),
-                                    lhsT_scale=x_scales[:, nt, x_place, :],
-                                    rhs=w_codes[place][:, slot, :].bitcast(FP8X4),
-                                    rhs_scale=w_scales[place][:, slot, :],
-                                    start=(slot == 0),
-                                    stop=(slot == len(taps) - 1),
-                                )
-                        places = slice(h * SIDE, (h + 1) * SIDE)
-                        nc.vector.tensor_tensor(
-                            out=biased[:, places, :], in0=acc[:], in1=bias_all[:, places, o_cols], op=ALU.add
-                        )
-                    by_channel = biased[:].rearrange("p s o -> p o s")
-                    final = result.tile([P, O_BLOCK, PLACES], F32)
-                    nc.vector.scalar_tensor_tensor(
-                        out=final[:], in0=by_channel, scalar=NEG_SLOPE, in1=by_channel, op0=ALU.mult, op1=ALU.max
+                biased = sums.tile([P, PLACES, O_BLOCK], F32)
+                for h in range(SIDE):
+                    acc = psum_acc.tile([P, SIDE, O_BLOCK], F32)
+                    for w in range(SIDE):
+                        place = h * SIDE + w
+                        taps = [(i, j) for i in taps_inside(h) for j in taps_inside(w)]
+                        for slot, (i, j) in enumerate(taps):
+                            x_place = (h + i - PAD) * SIDE + (w + j - PAD)
+                            nc.tensor.matmul_mx(
+                                out=acc[:, w, :],
+                                lhsT=x_codes[:, nt, x_place, :].bitcast(FP8X4),
+                                lhsT_scale=x_scales[:, nt, x_place, :],
+                                rhs=w_codes[place][:, slot, :].bitcast(FP8X4),
+                                rhs_scale=w_scales[place][:, slot, :],
+                                start=(slot == 0),
+                                stop=(slot == len(taps) - 1),
+                            )
+                    places = slice(h * SIDE, (h + 1) * SIDE)
+                    nc.vector.tensor_tensor(
+                        out=biased[:, places, :], in0=acc[:], in1=bias_all[:, places, o_cols], op=ALU.add
                     )
-                    nc.gpsimd.dma_start(out=out_rows[nt * P : (nt + 1) * P, o_cols], in_=final[:])
+                by_channel = biased[:].rearrange("p s o -> p o s")
+                final = result.tile([P, O_BLOCK, PLACES], F32)
+                nc.vector.scalar_tensor_tensor(
+                    out=final[:], in0=by_channel, scalar=NEG_SLOPE, in1=by_channel, op0=ALU.mult, op1=ALU.max
+                )
+                return final
+
+            def store(block, nt, final):
+                o_cols = slice(block * O_BLOCK, (block + 1) * O_BLOCK)
+                nc.sync.dma_start(out=out_rows[nt * P : (nt + 1) * P, o_cols], in_=final[:])
+
+            waiting = []
+            block_words = None
+            for block in range(O_BLOCKS):
+                w_grouped = []
+                for place in range(PLACES):
+                    n_taps = len(taps_inside(place // SIDE)) * len(taps_inside(place % SIDE))
+                    w_grouped.append(
+                        w_group.tile([P, n_taps, O_BLOCK, PACK], BF16, name="w_grouped%d" % place, align_bytes=64)
+                    )
+                for chunk in range(CHUNKS):
+                    k = block * CHUNKS + chunk
+                    if k + W_BUFFERS - 1 < O_BLOCKS * CHUNKS:
+                        load_weights(k + W_BUFFERS - 1)
+                    regroup(k, w_grouped)
+                    if block > 0 and chunk % (CHUNKS // N_TILES) == 0:
+                        nt = chunk // (CHUNKS // N_TILES)
+                        waiting.append((block - 1, nt, products(block - 1, nt, block_words[0], block_words[1])))
+                block_words = quantise(w_grouped)
+            for block, nt, final in waiting:
+                store(block, nt, final)
+            for nt in range(N_TILES):
+                store(O_BLOCKS - 1, nt, products(O_BLOCKS - 1, nt, block_words[0], block_words[1]))

@@ -23,6 +23,8 @@ O_BLOCKS = O // O_BLOCK
 O_CHUNK = 16
 CHUNKS = O_BLOCK // O_CHUNK
 W_BUFFERS = 6
+W_RUN = PACK * PLACES * TAPS
+W_PITCH = 336
 MAX_TAPS_PER_QUANTISE = 8
 
 USED_TAPS = 49
@@ -38,7 +40,7 @@ def tile_locallyconnected2d_t_kernel(tc, x, weight, bias, out):
     nc = tc.nc
 
     x_rows = x.rearrange("n c h w -> n c (h w)")
-    w_rows = weight.rearrange("a o (p t) h w k -> p (a o) t (h w k)", t=PACK)
+    w_rows = weight.rearrange("a o (p t) h w k -> p (a o) (t h w k)", t=PACK)
     bias_row = bias.rearrange("a o h w -> (a o h w)")
     out_rows = out.rearrange("n o h w -> n o (h w)")
 
@@ -58,8 +60,8 @@ def tile_locallyconnected2d_t_kernel(tc, x, weight, bias, out):
         w_raw = []
 
         def load_weights(k):
-            w_raw.append(w_load.tile([P, O_CHUNK, PACK, PLACES * TAPS], BF16, name="w_raw", tag="w_raw"))
-            nc.sync.dma_start(out=w_raw[k][:], in_=w_rows[:, k * O_CHUNK : (k + 1) * O_CHUNK])
+            w_raw.append(w_load.tile([P, O_CHUNK, W_PITCH], BF16, name="w_raw", tag="w_raw"))
+            nc.sync.dma_start(out=w_raw[k][:, :, 0:W_RUN], in_=w_rows[:, k * O_CHUNK : (k + 1) * O_CHUNK])
 
         x_codes = keep.tile([P, N_TILES, PLACES, P], U32, align_bytes=64)
         x_scales = keep.tile([P, N_TILES, PLACES, P], U8, align_bytes=64)
@@ -109,6 +111,7 @@ def tile_locallyconnected2d_t_kernel(tc, x, weight, bias, out):
 
             def regroup(k, w_grouped):
                 o_cols = slice((k % CHUNKS) * O_CHUNK, (k % CHUNKS + 1) * O_CHUNK)
+                by_tap = w_raw[k][:, :, 0:W_RUN].rearrange("p o (t f) -> p o t f", t=PACK)
                 for place in range(PLACES):
                     h, w = place // SIDE, place % SIDE
                     copy = nc.vector.tensor_copy if h == 1 else nc.scalar.copy
@@ -118,7 +121,7 @@ def tile_locallyconnected2d_t_kernel(tc, x, weight, bias, out):
                         slot = r * len(cols)
                         copy(
                             out=w_grouped[place][:, slot : slot + len(cols), o_cols, :].rearrange("p j o t -> p o j t"),
-                            in_=w_raw[k][:, :, :, f : f + len(cols)].rearrange("p o t j -> p o j t"),
+                            in_=by_tap[:, :, :, f : f + len(cols)].rearrange("p o t j -> p o j t"),
                         )
 
             def quantise(w_grouped):

@@ -114,7 +114,7 @@ def tile_locallyconnected2d_t_kernel(tc, x, weight, bias, out):
                 by_tap = w_raw[k][:, :, 0:W_RUN].rearrange("p o (t f) -> p o t f", t=PACK)
                 for place in range(PLACES):
                     h, w = place // SIDE, place % SIDE
-                    copy = nc.vector.tensor_copy if h == 1 else nc.scalar.copy
+                    copy = nc.scalar.copy if h == 1 else nc.vector.tensor_copy
                     cols = taps_inside(w)
                     for r, i in enumerate(taps_inside(h)):
                         f = place * TAPS + i * SIDE + cols[0]

@@ -23,6 +23,7 @@ O_BLOCKS = O // O_BLOCK
 O_CHUNK = 16
 CHUNKS = O_BLOCK // O_CHUNK
 W_BUFFERS = 6
+RUNS_PER_LOAD = 4
 W_RUN = PACK * PLACES * TAPS
 W_PITCH = 336
 MAX_TAPS_PER_QUANTISE = 8
@@ -61,7 +62,11 @@ def tile_locallyconnected2d_t_kernel(tc, x, weight, bias, out):
 
         def load_weights(k):
             w_raw.append(w_load.tile([P, O_CHUNK, W_PITCH], BF16, name="w_raw", tag="w_raw"))
-            nc.sync.dma_start(out=w_raw[k][:, :, 0:W_RUN], in_=w_rows[:, k * O_CHUNK : (k + 1) * O_CHUNK])
+            for first in range(0, O_CHUNK, RUNS_PER_LOAD):
+                nc.sync.dma_start(
+                    out=w_raw[k][:, first : first + RUNS_PER_LOAD, 0:W_RUN],
+                    in_=w_rows[:, k * O_CHUNK + first : k * O_CHUNK + first + RUNS_PER_LOAD],
+                )
 
         x_codes = keep.tile([P, N_TILES, PLACES, P], U32, align_bytes=64)
         x_scales = keep.tile([P, N_TILES, PLACES, P], U8, align_bytes=64)

@@ -23,9 +23,9 @@ O_BLOCKS = O // O_BLOCK
 O_CHUNK = 16
 CHUNKS = O_BLOCK // O_CHUNK
 W_BUFFERS = 6
-RUNS_PER_LOAD = 4
 W_RUN = PACK * PLACES * TAPS
 W_PITCH = 336
+W_LOADED = 320
 MAX_TAPS_PER_QUANTISE = 8
 
 USED_TAPS = 49
@@ -62,11 +62,7 @@ def tile_locallyconnected2d_t_kernel(tc, x, weight, bias, out):
 
         def load_weights(k):
             w_raw.append(w_load.tile([P, O_CHUNK, W_PITCH], BF16, name="w_raw", tag="w_raw"))
-            for first in range(0, O_CHUNK, RUNS_PER_LOAD):
-                nc.sync.dma_start(
-                    out=w_raw[k][:, first : first + RUNS_PER_LOAD, 0:W_RUN],
-                    in_=w_rows[:, k * O_CHUNK + first : k * O_CHUNK + first + RUNS_PER_LOAD],
-                )
+            nc.sync.dma_start(out=w_raw[k][:, :, 0:W_LOADED], in_=w_rows[:, k * O_CHUNK : (k + 1) * O_CHUNK, 0:W_LOADED])
 
         x_codes = keep.tile([P, N_TILES, PLACES, P], U32, align_bytes=64)
         x_scales = keep.tile([P, N_TILES, PLACES, P], U8, align_bytes=64)

@@ -26,7 +26,10 @@ W_BUFFERS = 6
 W_RUN = PACK * PLACES * TAPS
 W_PITCH = 336
 W_LOADED = 320
-MAX_TAPS_PER_QUANTISE = 8
+MAX_PLACES_PER_QUANTISE = 8
+O_HALF = O_BLOCK // 2
+
+assert N_TILES <= CHUNKS // 2
 
 USED_TAPS = 49
 FLOPS = 2 * N * C * O * USED_TAPS
@@ -47,9 +50,7 @@ def tile_locallyconnected2d_t_kernel(tc, x, weight, bias, out):
 
     with tc.manual_schedule(), tc.tile_pool(name="keep", bufs=1) as keep, tc.tile_pool(
         name="w_load", bufs=W_BUFFERS
-    ) as w_load, tc.tile_pool(name="w_group", bufs=1) as w_group, tc.psum_pool(
-        name="psum_x", bufs=3
-    ) as psum_x, tc.psum_pool(name="psum_acc", bufs=4) as psum_acc:
+    ) as w_load, tc.tile_pool(name="w_group", bufs=1) as w_group:
         identity = keep.tile([P, P], F32)
         make_identity(nc, identity[:])
 
@@ -66,7 +67,9 @@ def tile_locallyconnected2d_t_kernel(tc, x, weight, bias, out):
 
         x_codes = keep.tile([P, N_TILES, PLACES, P], U32, align_bytes=64)
         x_scales = keep.tile([P, N_TILES, PLACES, P], U8, align_bytes=64)
-        with tc.tile_pool(name="x_load", bufs=N_TILES) as x_load, tc.tile_pool(name="x_stage", bufs=2) as x_stage:
+        with tc.tile_pool(name="x_load", bufs=N_TILES) as x_load, tc.tile_pool(
+            name="x_stage", bufs=2
+        ) as x_stage, tc.psum_pool(name="psum_x", bufs=4) as psum_x:
             x_raw = []
             for nt in range(N_TILES):
                 x_raw.append(x_load.tile([P, C, PLACES], BF16, name="x_raw", tag="x_raw"))
@@ -80,8 +83,9 @@ def tile_locallyconnected2d_t_kernel(tc, x, weight, bias, out):
                 x_sorted.append(x_stage.tile([P, PLACES, C], BF16, name="x_sorted", tag="x_sorted"))
                 for row in range(SIDE):
                     places = slice(row * SIDE, (row + 1) * SIDE)
-                    copy = nc.scalar.copy if row == SIDE - 1 else nc.vector.tensor_copy
-                    copy(out=x_sorted[nt][:, places, :].rearrange("p s c -> p c s"), in_=x_raw[nt][:, :, places])
+                    nc.vector.tensor_copy(
+                        out=x_sorted[nt][:, places, :].rearrange("p s c -> p c s"), in_=x_raw[nt][:, :, places]
+                    )
 
             sort_by_place(0)
             for nt in range(N_TILES):
@@ -93,12 +97,11 @@ def tile_locallyconnected2d_t_kernel(tc, x, weight, bias, out):
                     x_t = psum_x.tile([P, 2, P], F32)
                     for u in range(2):
                         nc.tensor.transpose(x_t[:, u, :], words[:, u, :], identity[:])
-                    copy = nc.scalar.copy if s % 2 == 1 else nc.vector.tensor_copy
-                    copy(out=x_grouped[:, s, :, :], in_=x_t[:].rearrange("p u n -> p n u"))
+                    nc.scalar.copy(out=x_grouped[:, s, :, :], in_=x_t[:].rearrange("p u n -> p n u"))
 
                 first = 0
                 while first < PLACES:
-                    count = min(MAX_TAPS_PER_QUANTISE, PLACES - first)
+                    count = min(MAX_PLACES_PER_QUANTISE, PLACES - first)
                     nc.vector.quantize_mx(
                         out=x_codes[:, nt, first : first + count, :].rearrange("p s n -> p (s n)").bitcast(FP8X4),
                         scales=x_scales[:, nt, first : first + count, :].rearrange("p s n -> p (s n)"),
@@ -108,7 +111,7 @@ def tile_locallyconnected2d_t_kernel(tc, x, weight, bias, out):
 
         with tc.tile_pool(name="w_words", bufs=1) as w_words, tc.tile_pool(
             name="sums", bufs=2
-        ) as sums, tc.tile_pool(name="result", bufs=N_TILES) as result:
+        ) as sums, tc.tile_pool(name="result", bufs=N_TILES) as result, tc.psum_pool(name="psum_acc", bufs=6) as psum_acc:
 
             def regroup(k, w_grouped):
                 o_cols = slice((k % CHUNKS) * O_CHUNK, (k % CHUNKS + 1) * O_CHUNK)
@@ -125,27 +128,15 @@ def tile_locallyconnected2d_t_kernel(tc, x, weight, bias, out):
                             in_=by_tap[:, :, :, f : f + len(cols)].rearrange("p o t j -> p o j t"),
                         )
 
-            def quantise(w_grouped):
-                w_codes = []
-                w_scales = []
+            def quantise(w_grouped, w_codes, w_scales, half):
+                o_cols = slice(half * O_HALF, (half + 1) * O_HALF)
                 for place in range(PLACES):
-                    n_taps = w_grouped[place].shape[1]
-                    codes = w_words.tile([P, n_taps, O_BLOCK], U32, name="w_codes%d" % place, align_bytes=64)
-                    scales = w_words.tile([P, n_taps, O_BLOCK], U8, name="w_scales%d" % place, align_bytes=64)
-                    first = 0
-                    while first < n_taps:
-                        count = MAX_TAPS_PER_QUANTISE
-                        while count > n_taps - first:
-                            count //= 2
+                    for slot in range(w_grouped[place].shape[1]):
                         nc.vector.quantize_mx(
-                            out=codes[:, first : first + count, :].rearrange("p j o -> p (j o)").bitcast(FP8X4),
-                            scales=scales[:, first : first + count, :].rearrange("p j o -> p (j o)"),
-                            in_=w_grouped[place][:, first : first + count, :, :].rearrange("p j o t -> p (j o t)"),
+                            out=w_codes[place][:, slot, o_cols].bitcast(FP8X4),
+                            scales=w_scales[place][:, slot, o_cols],
+                            in_=w_grouped[place][:, slot, o_cols, :].rearrange("p o t -> p (o t)"),
                         )
-                        first += count
-                    w_codes.append(codes)
-                    w_scales.append(scales)
-                return w_codes, w_scales
 
             def products(block, nt, w_codes, w_scales):
                 o_cols = slice(block * O_BLOCK, (block + 1) * O_BLOCK)
@@ -170,11 +161,12 @@ def tile_locallyconnected2d_t_kernel(tc, x, weight, bias, out):
                     nc.vector.tensor_tensor(
                         out=biased[:, places, :], in0=acc[:], in1=bias_all[:, places, o_cols], op=ALU.add
                     )
-                by_channel = biased[:].rearrange("p s o -> p o s")
-                final = result.tile([P, O_BLOCK, PLACES], F32)
+                activated = sums.tile([P, PLACES, O_BLOCK], F32)
                 nc.vector.scalar_tensor_tensor(
-                    out=final[:], in0=by_channel, scalar=NEG_SLOPE, in1=by_channel, op0=ALU.mult, op1=ALU.max
+                    out=activated[:], in0=biased[:], scalar=NEG_SLOPE, in1=biased[:], op0=ALU.mult, op1=ALU.max
                 )
+                final = result.tile([P, O_BLOCK, PLACES], F32)
+                nc.scalar.copy(out=final[:], in_=activated[:].rearrange("p s o -> p o s"))
                 return final
 
             def store(block, nt, final):
@@ -182,7 +174,8 @@ def tile_locallyconnected2d_t_kernel(tc, x, weight, bias, out):
                 nc.sync.dma_start(out=out_rows[nt * P : (nt + 1) * P, o_cols], in_=final[:])
 
             waiting = []
-            block_words = None
+            w_codes = []
+            w_scales = []
             for block in range(O_BLOCKS):
                 w_grouped = []
                 for place in range(PLACES):
@@ -195,11 +188,22 @@ def tile_locallyconnected2d_t_kernel(tc, x, weight, bias, out):
                     if k + W_BUFFERS - 1 < O_BLOCKS * CHUNKS:
                         load_weights(k + W_BUFFERS - 1)
                     regroup(k, w_grouped)
-                    if block > 0 and chunk % (CHUNKS // N_TILES) == 0:
-                        nt = chunk // (CHUNKS // N_TILES)
-                        waiting.append((block - 1, nt, products(block - 1, nt, block_words[0], block_words[1])))
-                block_words = quantise(w_grouped)
+                    if block > 0 and chunk < N_TILES:
+                        waiting.append((block - 1, chunk, products(block - 1, chunk, w_codes, w_scales)))
+                    if chunk == CHUNKS // 2 - 1:
+                        w_codes = []
+                        w_scales = []
+                        for place in range(PLACES):
+                            n_taps = w_grouped[place].shape[1]
+                            w_codes.append(
+                                w_words.tile([P, n_taps, O_BLOCK], U32, name="w_codes%d" % place, align_bytes=64)
+                            )
+                            w_scales.append(
+                                w_words.tile([P, n_taps, O_BLOCK], U8, name="w_scales%d" % place, align_bytes=64)
+                            )
+                        quantise(w_grouped, w_codes, w_scales, 0)
+                quantise(w_grouped, w_codes, w_scales, 1)
             for block, nt, final in waiting:
                 store(block, nt, final)
             for nt in range(N_TILES):
-                store(O_BLOCKS - 1, nt, products(O_BLOCKS - 1, nt, block_words[0], block_words[1]))
+                store(O_BLOCKS - 1, nt, products(O_BLOCKS - 1, nt, w_codes, w_scales))

@@ -45,7 +45,7 @@ def tile_locallyconnected2d_t_kernel(tc, x, weight, bias, out):
 
     x_rows = x.rearrange("n c h w -> n c (h w)")
     w_rows = weight.rearrange("a o (p t) h w k -> p (a o) (t h w k)", t=PACK)
-    bias_row = bias.rearrange("a o h w -> (a o h w)")
+    bias_row = bias.rearrange("a o h w -> a (o h w)")
     out_rows = out.rearrange("n o h w -> n o (h w)")
 
     with tc.manual_schedule(), tc.tile_pool(name="keep", bufs=1) as keep, tc.tile_pool(
@@ -54,10 +54,12 @@ def tile_locallyconnected2d_t_kernel(tc, x, weight, bias, out):
         identity = keep.tile([P, P], F32)
         make_identity(nc, identity[:])
 
-        bias_raw = keep.tile([P, O, PLACES], BF16)
-        nc.gpsimd.dma_start(out=bias_raw[:].rearrange("p o s -> p (o s)"), in_=bias_row.partition_broadcast(P))
+        bias_rows = keep.tile([P, O, PLACES], BF16)
+        nc.vector.memset(bias_rows[:], 0.0)
+        nc.gpsimd.dma_start(out=bias_rows[0:1].rearrange("p o s -> p (o s)"), in_=bias_row)
+        ones = keep.tile([P, P], BF16)
+        nc.vector.memset(ones[:], 1.0)
         bias_all = keep.tile([P, PLACES, O], F32)
-        nc.gpsimd.tensor_copy(out=bias_all[:], in_=bias_raw[:].rearrange("p o s -> p s o"))
 
         w_raw = []
 
@@ -108,6 +110,11 @@ def tile_locallyconnected2d_t_kernel(tc, x, weight, bias, out):
                         in_=x_grouped[:, first : first + count, :, :].rearrange("p s n u -> p (s n u)").bitcast(BF16),
                     )
                     first += count
+
+            for s in range(PLACES):
+                spread = psum_x.tile([P, O], F32)
+                nc.tensor.matmul(spread[:], lhsT=ones[:], rhs=bias_rows[:, :, s], start=True, stop=True)
+                nc.scalar.copy(out=bias_all[:, s, :], in_=spread[:])
 
         with tc.tile_pool(name="w_words", bufs=1) as w_words, tc.tile_pool(
             name="sums", bufs=2

@@ -30,6 +30,8 @@ MAX_PLACES_PER_QUANTISE = 8
 O_HALF = O_BLOCK // 2
 
 assert N_TILES <= CHUNKS // 2
+BIAS_AFTER_CHUNK = 2
+ROW_ORDER = (0, 2, 1)
 
 USED_TAPS = 49
 FLOPS = 2 * N * C * O * USED_TAPS
@@ -111,11 +113,6 @@ def tile_locallyconnected2d_t_kernel(tc, x, weight, bias, out):
                     )
                     first += count
 
-            for s in range(PLACES):
-                spread = psum_x.tile([P, O], F32)
-                nc.tensor.matmul(spread[:], lhsT=ones[:], rhs=bias_rows[:, :, s], start=True, stop=True)
-                nc.scalar.copy(out=bias_all[:, s, :], in_=spread[:])
-
         with tc.tile_pool(name="w_words", bufs=1) as w_words, tc.tile_pool(
             name="sums", bufs=2
         ) as sums, tc.tile_pool(name="result", bufs=N_TILES) as result, tc.psum_pool(name="psum_acc", bufs=6) as psum_acc:
@@ -137,7 +134,7 @@ def tile_locallyconnected2d_t_kernel(tc, x, weight, bias, out):
 
             def quantise(w_grouped, w_codes, w_scales, half):
                 o_cols = slice(half * O_HALF, (half + 1) * O_HALF)
-                for place in range(PLACES):
+                for place in [h * SIDE + w for h in ROW_ORDER for w in range(SIDE)]:
                     for slot in range(w_grouped[place].shape[1]):
                         nc.vector.quantize_mx(
                             out=w_codes[place][:, slot, o_cols].bitcast(FP8X4),
@@ -145,10 +142,9 @@ def tile_locallyconnected2d_t_kernel(tc, x, weight, bias, out):
                             in_=w_grouped[place][:, slot, o_cols, :].rearrange("p o t -> p (o t)"),
                         )
 
-            def products(block, nt, w_codes, w_scales):
-                o_cols = slice(block * O_BLOCK, (block + 1) * O_BLOCK)
-                biased = sums.tile([P, PLACES, O_BLOCK], F32)
-                for h in range(SIDE):
+            def passes(nt, w_codes, w_scales):
+                banks = []
+                for h in ROW_ORDER:
                     acc = psum_acc.tile([P, SIDE, O_BLOCK], F32)
                     for w in range(SIDE):
                         place = h * SIDE + w
@@ -164,6 +160,13 @@ def tile_locallyconnected2d_t_kernel(tc, x, weight, bias, out):
                                 start=(slot == 0),
                                 stop=(slot == len(taps) - 1),
                             )
+                    banks.append((h, acc))
+                return banks
+
+            def activate(block, banks):
+                o_cols = slice(block * O_BLOCK, (block + 1) * O_BLOCK)
+                biased = sums.tile([P, PLACES, O_BLOCK], F32)
+                for h, acc in banks:
                     places = slice(h * SIDE, (h + 1) * SIDE)
                     nc.vector.tensor_tensor(
                         out=biased[:, places, :], in0=acc[:], in1=bias_all[:, places, o_cols], op=ALU.add
@@ -172,6 +175,9 @@ def tile_locallyconnected2d_t_kernel(tc, x, weight, bias, out):
                 nc.vector.scalar_tensor_tensor(
                     out=activated[:], in0=biased[:], scalar=NEG_SLOPE, in1=biased[:], op0=ALU.mult, op1=ALU.max
                 )
+                return activated
+
+            def interleave(activated):
                 final = result.tile([P, O_BLOCK, PLACES], F32)
                 nc.scalar.copy(out=final[:], in_=activated[:].rearrange("p s o -> p o s"))
                 return final
@@ -181,6 +187,8 @@ def tile_locallyconnected2d_t_kernel(tc, x, weight, bias, out):
                 nc.sync.dma_start(out=out_rows[nt * P : (nt + 1) * P, o_cols], in_=final[:])
 
             waiting = []
+            banks_before = None
+            activated_before = None
             w_codes = []
             w_scales = []
             for block in range(O_BLOCKS):
@@ -195,9 +203,20 @@ def tile_locallyconnected2d_t_kernel(tc, x, weight, bias, out):
                     if k + W_BUFFERS - 1 < O_BLOCKS * CHUNKS:
                         load_weights(k + W_BUFFERS - 1)
                     regroup(k, w_grouped)
+                    if k == BIAS_AFTER_CHUNK:
+                        for s in range(PLACES):
+                            spread = psum_acc.tile([P, O], F32, name="acc")
+                            nc.tensor.matmul(spread[:], lhsT=ones[:], rhs=bias_rows[:, :, s], start=True, stop=True)
+                            nc.scalar.copy(out=bias_all[:, s, :], in_=spread[:])
+                    if activated_before is not None:
+                        waiting.append((block - 1, activated_before[0], interleave(activated_before[1])))
+                        activated_before = None
+                    if banks_before is not None:
+                        activated_before = (banks_before[0], activate(block - 1, banks_before[1]))
+                        banks_before = None
                     if block > 0 and chunk < N_TILES:
-                        waiting.append((block - 1, chunk, products(block - 1, chunk, w_codes, w_scales)))
-                    if chunk == CHUNKS // 2 - 1:
+                        banks_before = (chunk, passes(chunk, w_codes, w_scales))
+                    if chunk == CHUNKS // 2:
                         w_codes = []
                         w_scales = []
                         for place in range(PLACES):
@@ -213,4 +232,4 @@ def tile_locallyconnected2d_t_kernel(tc, x, weight, bias, out):
             for block, nt, final in waiting:
                 store(block, nt, final)
             for nt in range(N_TILES):
-                store(O_BLOCKS - 1, nt, products(O_BLOCKS - 1, nt, w_codes, w_scales))
+                store(O_BLOCKS - 1, nt, interleave(activate(O_BLOCKS - 1, passes(nt, w_codes, w_scales))))

@@ -115,7 +115,7 @@ def tile_locallyconnected2d_t_kernel(tc, x, weight, bias, out):
 
         with tc.tile_pool(name="w_words", bufs=1) as w_words, tc.tile_pool(
             name="sums", bufs=2
-        ) as sums, tc.tile_pool(name="result", bufs=N_TILES) as result, tc.psum_pool(name="psum_acc", bufs=6) as psum_acc:
+        ) as sums, tc.tile_pool(name="rows", bufs=2) as rows, tc.tile_pool(name="result", bufs=N_TILES) as result, tc.psum_pool(name="psum_acc", bufs=6) as psum_acc:
 
             def regroup(k, w_grouped):
                 o_cols = slice((k % CHUNKS) * O_CHUNK, (k % CHUNKS + 1) * O_CHUNK)
@@ -142,9 +142,9 @@ def tile_locallyconnected2d_t_kernel(tc, x, weight, bias, out):
                             in_=w_grouped[place][:, slot, o_cols, :].rearrange("p o t -> p (o t)"),
                         )
 
-            def passes(nt, w_codes, w_scales):
+            def passes(nt, w_codes, w_scales, row_order):
                 banks = []
-                for h in ROW_ORDER:
+                for h in row_order:
                     acc = psum_acc.tile([P, SIDE, O_BLOCK], F32)
                     for w in range(SIDE):
                         place = h * SIDE + w
@@ -215,7 +215,7 @@ def tile_locallyconnected2d_t_kernel(tc, x, weight, bias, out):
                         activated_before = (banks_before[0], activate(block - 1, banks_before[1]))
                         banks_before = None
                     if block > 0 and chunk < N_TILES:
-                        banks_before = (chunk, passes(chunk, w_codes, w_scales))
+                        banks_before = (chunk, passes(chunk, w_codes, w_scales, ROW_ORDER))
                     if chunk == CHUNKS // 2:
                         w_codes = []
                         w_scales = []
@@ -231,5 +231,19 @@ def tile_locallyconnected2d_t_kernel(tc, x, weight, bias, out):
                 quantise(w_grouped, w_codes, w_scales, 1)
             for block, nt, final in waiting:
                 store(block, nt, final)
-            for nt in range(N_TILES):
-                store(O_BLOCKS - 1, nt, interleave(activate(O_BLOCKS - 1, passes(nt, w_codes, w_scales))))
+            for nt in range(N_TILES - 1):
+                store(O_BLOCKS - 1, nt, interleave(activate(O_BLOCKS - 1, passes(nt, w_codes, w_scales, ROW_ORDER))))
+            o_cols = slice((O_BLOCKS - 1) * O_BLOCK, O_BLOCKS * O_BLOCK)
+            final = result.tile([P, O_BLOCK, PLACES], F32)
+            for h in ROW_ORDER:
+                places = slice(h * SIDE, (h + 1) * SIDE)
+                acc = passes(N_TILES - 1, w_codes, w_scales, (h,))[0][1]
+                biased_row = rows.tile([P, SIDE, O_BLOCK], F32)
+                nc.vector.tensor_tensor(out=biased_row[:], in0=acc[:], in1=bias_all[:, places, o_cols], op=ALU.add)
+                activated_row = rows.tile([P, SIDE, O_BLOCK], F32)
+                nc.vector.scalar_tensor_tensor(
+                    out=activated_row[:], in0=biased_row[:], scalar=NEG_SLOPE, in1=biased_row[:], op0=ALU.mult, op1=ALU.max
+                )
+                copy = nc.vector.tensor_copy if h == ROW_ORDER[-1] else nc.scalar.copy
+                copy(out=final[:, :, places], in_=activated_row[:].rearrange("p w o -> p o w"))
+            store(O_BLOCKS - 1, N_TILES - 1, final)

@@ -61,7 +61,7 @@ def tile_locallyconnected2d_t_kernel(tc, x, weight, bias, out):
         nc.gpsimd.dma_start(out=bias_rows[0:1].rearrange("p o s -> p (o s)"), in_=bias_row)
         ones = keep.tile([P, P], BF16)
         nc.vector.memset(ones[:], 1.0)
-        bias_all = keep.tile([P, PLACES, O], F32)
+        bias_all = keep.tile([P, SIDE, O_BLOCKS, O_BLOCK, SIDE], F32)
 
         w_raw = []
 
@@ -120,9 +120,9 @@ def tile_locallyconnected2d_t_kernel(tc, x, weight, bias, out):
             def regroup(k, w_grouped):
                 o_cols = slice((k % CHUNKS) * O_CHUNK, (k % CHUNKS + 1) * O_CHUNK)
                 by_tap = w_raw[k][:, :, 0:W_RUN].rearrange("p o (t f) -> p o t f", t=PACK)
-                for place in range(PLACES):
+                for place in [h * SIDE + w for h in ROW_ORDER for w in range(SIDE)]:
                     h, w = place // SIDE, place % SIDE
-                    copy = nc.scalar.copy if h == 1 else nc.vector.tensor_copy
+                    copy = nc.scalar.copy if h == 1 or place == PLACES - 1 else nc.vector.tensor_copy
                     cols = taps_inside(w)
                     for r, i in enumerate(taps_inside(h)):
                         f = place * TAPS + i * SIDE + cols[0]
@@ -164,14 +164,15 @@ def tile_locallyconnected2d_t_kernel(tc, x, weight, bias, out):
                 return banks
 
             def activate(block, banks):
-                o_cols = slice(block * O_BLOCK, (block + 1) * O_BLOCK)
-                biased = sums.tile([P, PLACES, O_BLOCK], F32)
+                biased = sums.tile([P, SIDE, O_BLOCK, SIDE], F32)
                 for h, acc in banks:
-                    places = slice(h * SIDE, (h + 1) * SIDE)
                     nc.vector.tensor_tensor(
-                        out=biased[:, places, :], in0=acc[:], in1=bias_all[:, places, o_cols], op=ALU.add
+                        out=biased[:, h, :, :],
+                        in0=acc[:].rearrange("p w o -> p o w"),
+                        in1=bias_all[:, h, block, :, :],
+                        op=ALU.add,
                     )
-                activated = sums.tile([P, PLACES, O_BLOCK], F32)
+                activated = sums.tile([P, SIDE, O_BLOCK, SIDE], F32)
                 nc.vector.scalar_tensor_tensor(
                     out=activated[:], in0=biased[:], scalar=NEG_SLOPE, in1=biased[:], op0=ALU.mult, op1=ALU.max
                 )
@@ -179,7 +180,9 @@ def tile_locallyconnected2d_t_kernel(tc, x, weight, bias, out):
 
             def interleave(activated):
                 final = result.tile([P, O_BLOCK, PLACES], F32)
-                nc.scalar.copy(out=final[:], in_=activated[:].rearrange("p s o -> p o s"))
+                nc.scalar.copy(
+                    out=final[:].rearrange("p o (h w) -> p o h w", h=SIDE), in_=activated[:].rearrange("p h o w -> p o h w")
+                )
                 return final
 
             def store(block, nt, final):
@@ -204,10 +207,17 @@ def tile_locallyconnected2d_t_kernel(tc, x, weight, bias, out):
                         load_weights(k + W_BUFFERS - 1)
                     regroup(k, w_grouped)
                     if k == BIAS_AFTER_CHUNK:
-                        for s in range(PLACES):
-                            spread = psum_acc.tile([P, O], F32, name="acc")
-                            nc.tensor.matmul(spread[:], lhsT=ones[:], rhs=bias_rows[:, :, s], start=True, stop=True)
-                            nc.scalar.copy(out=bias_all[:, s, :], in_=spread[:])
+                        for h in range(SIDE):
+                            for b in range(O_BLOCKS):
+                                spread = psum_acc.tile([P, O_BLOCK, SIDE], F32, name="acc")
+                                nc.tensor.matmul(
+                                    spread[:],
+                                    lhsT=ones[:],
+                                    rhs=bias_rows[:, b * O_BLOCK : (b + 1) * O_BLOCK, h * SIDE : (h + 1) * SIDE],
+                                    start=True,
+                                    stop=True,
+                                )
+                                nc.scalar.copy(out=bias_all[:, h, b, :, :], in_=spread[:])
                     if activated_before is not None:
                         waiting.append((block - 1, activated_before[0], interleave(activated_before[1])))
                         activated_before = None
@@ -233,17 +243,21 @@ def tile_locallyconnected2d_t_kernel(tc, x, weight, bias, out):
                 store(block, nt, final)
             for nt in range(N_TILES - 1):
                 store(O_BLOCKS - 1, nt, interleave(activate(O_BLOCKS - 1, passes(nt, w_codes, w_scales, ROW_ORDER))))
-            o_cols = slice((O_BLOCKS - 1) * O_BLOCK, O_BLOCKS * O_BLOCK)
             final = result.tile([P, O_BLOCK, PLACES], F32)
             for h in ROW_ORDER:
                 places = slice(h * SIDE, (h + 1) * SIDE)
                 acc = passes(N_TILES - 1, w_codes, w_scales, (h,))[0][1]
-                biased_row = rows.tile([P, SIDE, O_BLOCK], F32)
-                nc.vector.tensor_tensor(out=biased_row[:], in0=acc[:], in1=bias_all[:, places, o_cols], op=ALU.add)
-                activated_row = rows.tile([P, SIDE, O_BLOCK], F32)
+                biased_row = rows.tile([P, O_BLOCK, SIDE], F32)
+                nc.vector.tensor_tensor(
+                    out=biased_row[:],
+                    in0=acc[:].rearrange("p w o -> p o w"),
+                    in1=bias_all[:, h, O_BLOCKS - 1, :, :],
+                    op=ALU.add,
+                )
+                activated_row = rows.tile([P, O_BLOCK, SIDE], F32)
                 nc.vector.scalar_tensor_tensor(
                     out=activated_row[:], in0=biased_row[:], scalar=NEG_SLOPE, in1=biased_row[:], op0=ALU.mult, op1=ALU.max
                 )
                 copy = nc.vector.tensor_copy if h == ROW_ORDER[-1] else nc.scalar.copy
-                copy(out=final[:, :, places], in_=activated_row[:].rearrange("p w o -> p o w"))
+                copy(out=final[:, :, places], in_=activated_row[:])
             store(O_BLOCKS - 1, N_TILES - 1, final)

@@ -65,9 +65,18 @@ def tile_locallyconnected2d_t_kernel(tc, x, weight, bias, out):
 
         w_raw = []
 
+        def parts_of(k):
+            if k == O_BLOCKS * CHUNKS - 1:
+                return [slice(0, O_CHUNK // 2), slice(O_CHUNK // 2, O_CHUNK)]
+            return [slice(0, O_CHUNK)]
+
         def load_weights(k):
             w_raw.append(w_load.tile([P, O_CHUNK, W_PITCH], BF16, name="w_raw", tag="w_raw"))
-            nc.sync.dma_start(out=w_raw[k][:, :, 0:W_LOADED], in_=w_rows[:, k * O_CHUNK : (k + 1) * O_CHUNK, 0:W_LOADED])
+            for part in parts_of(k):
+                nc.sync.dma_start(
+                    out=w_raw[k][:, part, 0:W_LOADED],
+                    in_=w_rows[:, k * O_CHUNK + part.start : k * O_CHUNK + part.stop, 0:W_LOADED],
+                )
 
         x_codes = keep.tile([P, N_TILES, PLACES, P], U32, align_bytes=64)
         x_scales = keep.tile([P, N_TILES, PLACES, P], U8, align_bytes=64)
@@ -118,19 +127,22 @@ def tile_locallyconnected2d_t_kernel(tc, x, weight, bias, out):
         ) as sums, tc.tile_pool(name="rows", bufs=2) as rows, tc.tile_pool(name="result", bufs=N_TILES) as result, tc.psum_pool(name="psum_acc", bufs=6) as psum_acc:
 
             def regroup(k, w_grouped):
-                o_cols = slice((k % CHUNKS) * O_CHUNK, (k % CHUNKS + 1) * O_CHUNK)
-                by_tap = w_raw[k][:, :, 0:W_RUN].rearrange("p o (t f) -> p o t f", t=PACK)
-                for place in [h * SIDE + w for h in ROW_ORDER for w in range(SIDE)]:
-                    h, w = place // SIDE, place % SIDE
-                    copy = nc.scalar.copy if h == 1 or place == PLACES - 1 else nc.vector.tensor_copy
-                    cols = taps_inside(w)
-                    for r, i in enumerate(taps_inside(h)):
-                        f = place * TAPS + i * SIDE + cols[0]
-                        slot = r * len(cols)
-                        copy(
-                            out=w_grouped[place][:, slot : slot + len(cols), o_cols, :].rearrange("p j o t -> p o j t"),
-                            in_=by_tap[:, :, :, f : f + len(cols)].rearrange("p o t j -> p o j t"),
-                        )
+                for part in parts_of(k):
+                    o_cols = slice((k % CHUNKS) * O_CHUNK + part.start, (k % CHUNKS) * O_CHUNK + part.stop)
+                    by_tap = w_raw[k][:, part, 0:W_RUN].rearrange("p o (t f) -> p o t f", t=PACK)
+                    for place in [h * SIDE + w for h in ROW_ORDER for w in range(SIDE)]:
+                        h, w = place // SIDE, place % SIDE
+                        copy = nc.scalar.copy if h == 1 or place == PLACES - 1 else nc.vector.tensor_copy
+                        cols = taps_inside(w)
+                        for r, i in enumerate(taps_inside(h)):
+                            f = place * TAPS + i * SIDE + cols[0]
+                            slot = r * len(cols)
+                            copy(
+                                out=w_grouped[place][:, slot : slot + len(cols), o_cols, :].rearrange(
+                                    "p j o t -> p o j t"
+                                ),
+                                in_=by_tap[:, :, :, f : f + len(cols)].rearrange("p o t j -> p o j t"),
+                            )
 
             def quantise(w_grouped, w_codes, w_scales, half):
                 o_cols = slice(half * O_HALF, (half + 1) * O_HALF)

import concourse.mybir as mybir
from concourse.masks import make_identity

BF16 = mybir.dt.bfloat16
F32 = mybir.dt.float32
U32 = mybir.dt.uint32
U8 = mybir.dt.uint8
FP8X4 = mybir.dt.float8_e4m3fn_x4
ALU = mybir.AluOpType

P = 128
PACK = 4
N, C, O = 512, 512, 256
SIDE = 3
PLACES = SIDE * SIDE
TAPS = SIDE * SIDE
PAD = 1
NEG_SLOPE = 0.1

N_TILES = N // P
O_BLOCK = 128
O_BLOCKS = O // O_BLOCK
O_CHUNK = 16
CHUNKS = O_BLOCK // O_CHUNK
W_BUFFERS = 6
W_RUN = PACK * PLACES * TAPS
W_PITCH = 336
W_LOADED = 320
MAX_PLACES_PER_QUANTISE = 8
O_HALF = O_BLOCK // 2

assert N_TILES <= CHUNKS // 2
BIAS_AFTER_CHUNK = 2
ROW_ORDER = (0, 2, 1)

USED_TAPS = 49
FLOPS = 2 * N * C * O * USED_TAPS
BYTES = 2 * N * C * PLACES + 2 * O * C * USED_TAPS + 2 * O * PLACES + 4 * N * O * PLACES


def taps_inside(coordinate):
    return range(max(0, PAD - coordinate), min(SIDE, SIDE + PAD - coordinate))


def tile_locallyconnected2d_t_kernel(tc, x, weight, bias, out):
    nc = tc.nc

    x_rows = x.rearrange("n c h w -> n c (h w)")
    w_rows = weight.rearrange("a o (p t) h w k -> p (a o) (t h w k)", t=PACK)
    bias_row = bias.rearrange("a o h w -> a (o h w)")
    out_rows = out.rearrange("n o h w -> n o (h w)")

    with tc.manual_schedule(), tc.tile_pool(name="keep", bufs=1) as keep, tc.tile_pool(
        name="w_load", bufs=W_BUFFERS
    ) as w_load, tc.tile_pool(name="w_group", bufs=1) as w_group:
        identity = keep.tile([P, P], F32)
        make_identity(nc, identity[:])

        bias_rows = keep.tile([P, O, PLACES], BF16)
        nc.vector.memset(bias_rows[:], 0.0)
        nc.gpsimd.dma_start(out=bias_rows[0:1].rearrange("p o s -> p (o s)"), in_=bias_row)
        ones = keep.tile([P, P], BF16)
        nc.vector.memset(ones[:], 1.0)
        bias_all = keep.tile([P, SIDE, O_BLOCKS, O_BLOCK, SIDE], F32)

        w_raw = []

        def parts_of(k):
            if k == O_BLOCKS * CHUNKS - 1:
                return [slice(0, O_CHUNK // 2), slice(O_CHUNK // 2, O_CHUNK)]
            return [slice(0, O_CHUNK)]

        def load_weights(k):
            w_raw.append(w_load.tile([P, O_CHUNK, W_PITCH], BF16, name="w_raw", tag="w_raw"))
            for part in parts_of(k):
                nc.sync.dma_start(
                    out=w_raw[k][:, part, 0:W_LOADED],
                    in_=w_rows[:, k * O_CHUNK + part.start : k * O_CHUNK + part.stop, 0:W_LOADED],
                )

        x_codes = keep.tile([P, N_TILES, PLACES, P], U32, align_bytes=64)
        x_scales = keep.tile([P, N_TILES, PLACES, P], U8, align_bytes=64)
        with tc.tile_pool(name="x_load", bufs=N_TILES) as x_load, tc.tile_pool(
            name="x_stage", bufs=2
        ) as x_stage, tc.psum_pool(name="psum_x", bufs=4) as psum_x:
            x_raw = []
            for nt in range(N_TILES):
                x_raw.append(x_load.tile([P, C, PLACES], BF16, name="x_raw", tag="x_raw"))
                nc.sync.dma_start(out=x_raw[nt][:], in_=x_rows[nt * P : (nt + 1) * P])
            for k in range(W_BUFFERS - 1):
                load_weights(k)

            x_sorted = []

            def sort_by_place(nt):
                x_sorted.append(x_stage.tile([P, PLACES, C], BF16, name="x_sorted", tag="x_sorted"))
                for row in range(SIDE):
                    places = slice(row * SIDE, (row + 1) * SIDE)
                    nc.vector.tensor_copy(
                        out=x_sorted[nt][:, places, :].rearrange("p s c -> p c s"), in_=x_raw[nt][:, :, places]
                    )

            sort_by_place(0)
            for nt in range(N_TILES):
                if nt + 1 < N_TILES:
                    sort_by_place(nt + 1)
                x_grouped = x_stage.tile([P, PLACES, P, 2], F32, align_bytes=64)
                for s in range(PLACES):
                    words = x_sorted[nt][:, s, :].bitcast(F32).rearrange("p (q u) -> p u q", u=2)
                    x_t = psum_x.tile([P, 2, P], F32)
                    for u in range(2):
                        nc.tensor.transpose(x_t[:, u, :], words[:, u, :], identity[:])
                    nc.scalar.copy(out=x_grouped[:, s, :, :], in_=x_t[:].rearrange("p u n -> p n u"))

                first = 0
                while first < PLACES:
                    count = min(MAX_PLACES_PER_QUANTISE, PLACES - first)
                    nc.vector.quantize_mx(
                        out=x_codes[:, nt, first : first + count, :].rearrange("p s n -> p (s n)").bitcast(FP8X4),
                        scales=x_scales[:, nt, first : first + count, :].rearrange("p s n -> p (s n)"),
                        in_=x_grouped[:, first : first + count, :, :].rearrange("p s n u -> p (s n u)").bitcast(BF16),
                    )
                    first += count

        with tc.tile_pool(name="w_words", bufs=1) as w_words, tc.tile_pool(
            name="sums", bufs=2
        ) as sums, tc.tile_pool(name="rows", bufs=2) as rows, tc.tile_pool(name="result", bufs=N_TILES) as result, tc.psum_pool(name="psum_acc", bufs=6) as psum_acc:

            def regroup(k, w_grouped):
                for part in parts_of(k):
                    o_cols = slice((k % CHUNKS) * O_CHUNK + part.start, (k % CHUNKS) * O_CHUNK + part.stop)
                    by_tap = w_raw[k][:, part, 0:W_RUN].rearrange("p o (t f) -> p o t f", t=PACK)
                    for place in [h * SIDE + w for h in ROW_ORDER for w in range(SIDE)]:
                        h, w = place // SIDE, place % SIDE
                        copy = nc.scalar.copy if h == 1 or place == PLACES - 1 else nc.vector.tensor_copy
                        cols = taps_inside(w)
                        for r, i in enumerate(taps_inside(h)):
                            f = place * TAPS + i * SIDE + cols[0]
                            slot = r * len(cols)
                            copy(
                                out=w_grouped[place][:, slot : slot + len(cols), o_cols, :].rearrange(
                                    "p j o t -> p o j t"
                                ),
                                in_=by_tap[:, :, :, f : f + len(cols)].rearrange("p o t j -> p o j t"),
                            )

            def quantise(w_grouped, w_codes, w_scales, half):
                o_cols = slice(half * O_HALF, (half + 1) * O_HALF)
                for place in [h * SIDE + w for h in ROW_ORDER for w in range(SIDE)]:
                    for slot in range(w_grouped[place].shape[1]):
                        nc.vector.quantize_mx(
                            out=w_codes[place][:, slot, o_cols].bitcast(FP8X4),
                            scales=w_scales[place][:, slot, o_cols],
                            in_=w_grouped[place][:, slot, o_cols, :].rearrange("p o t -> p (o t)"),
                        )

            def passes(nt, w_codes, w_scales, row_order):
                banks = []
                for h in row_order:
                    acc = psum_acc.tile([P, SIDE, O_BLOCK], F32)
                    for w in range(SIDE):
                        place = h * SIDE + w
                        taps = [(i, j) for i in taps_inside(h) for j in taps_inside(w)]
                        for slot, (i, j) in enumerate(taps):
                            x_place = (h + i - PAD) * SIDE + (w + j - PAD)
                            nc.tensor.matmul_mx(
                                out=acc[:, w, :],
                                lhsT=x_codes[:, nt, x_place, :].bitcast(FP8X4),
                                lhsT_scale=x_scales[:, nt, x_place, :],
                                rhs=w_codes[place][:, slot, :].bitcast(FP8X4),
                                rhs_scale=w_scales[place][:, slot, :],
                                start=(slot == 0),
                                stop=(slot == len(taps) - 1),
                            )
                    banks.append((h, acc))
                return banks

            def activate(block, banks):
                biased = sums.tile([P, SIDE, O_BLOCK, SIDE], F32)
                for h, acc in banks:
                    nc.vector.tensor_tensor(
                        out=biased[:, h, :, :],
                        in0=acc[:].rearrange("p w o -> p o w"),
                        in1=bias_all[:, h, block, :, :],
                        op=ALU.add,
                    )
                activated = sums.tile([P, SIDE, O_BLOCK, SIDE], F32)
                nc.vector.scalar_tensor_tensor(
                    out=activated[:], in0=biased[:], scalar=NEG_SLOPE, in1=biased[:], op0=ALU.mult, op1=ALU.max
                )
                return activated

            def interleave(activated):
                final = result.tile([P, O_BLOCK, PLACES], F32)
                nc.scalar.copy(
                    out=final[:].rearrange("p o (h w) -> p o h w", h=SIDE), in_=activated[:].rearrange("p h o w -> p o h w")
                )
                return final

            def store(block, nt, final):
                o_cols = slice(block * O_BLOCK, (block + 1) * O_BLOCK)
                nc.sync.dma_start(out=out_rows[nt * P : (nt + 1) * P, o_cols], in_=final[:])

            waiting = []
            banks_before = None
            activated_before = None
            w_codes = []
            w_scales = []
            for block in range(O_BLOCKS):
                w_grouped = []
                for place in range(PLACES):
                    n_taps = len(taps_inside(place // SIDE)) * len(taps_inside(place % SIDE))
                    w_grouped.append(
                        w_group.tile([P, n_taps, O_BLOCK, PACK], BF16, name="w_grouped%d" % place, align_bytes=64)
                    )
                for chunk in range(CHUNKS):
                    k = block * CHUNKS + chunk
                    if k + W_BUFFERS - 1 < O_BLOCKS * CHUNKS:
                        load_weights(k + W_BUFFERS - 1)
                    regroup(k, w_grouped)
                    if k == BIAS_AFTER_CHUNK:
                        for h in range(SIDE):
                            for b in range(O_BLOCKS):
                                spread = psum_acc.tile([P, O_BLOCK, SIDE], F32, name="acc")
                                nc.tensor.matmul(
                                    spread[:],
                                    lhsT=ones[:],
                                    rhs=bias_rows[:, b * O_BLOCK : (b + 1) * O_BLOCK, h * SIDE : (h + 1) * SIDE],
                                    start=True,
                                    stop=True,
                                )
                                nc.scalar.copy(out=bias_all[:, h, b, :, :], in_=spread[:])
                    if activated_before is not None:
                        waiting.append((block - 1, activated_before[0], interleave(activated_before[1])))
                        activated_before = None
                    if banks_before is not None:
                        activated_before = (banks_before[0], activate(block - 1, banks_before[1]))
                        banks_before = None
                    if block > 0 and chunk < N_TILES:
                        banks_before = (chunk, passes(chunk, w_codes, w_scales, ROW_ORDER))
                    if chunk == CHUNKS // 2:
                        w_codes = []
                        w_scales = []
                        for place in range(PLACES):
                            n_taps = w_grouped[place].shape[1]
                            w_codes.append(
                                w_words.tile([P, n_taps, O_BLOCK], U32, name="w_codes%d" % place, align_bytes=64)
                            )
                            w_scales.append(
                                w_words.tile([P, n_taps, O_BLOCK], U8, name="w_scales%d" % place, align_bytes=64)
                            )
                        quantise(w_grouped, w_codes, w_scales, 0)
                quantise(w_grouped, w_codes, w_scales, 1)
            for block, nt, final in waiting:
                store(block, nt, final)
            for nt in range(N_TILES - 1):
                store(O_BLOCKS - 1, nt, interleave(activate(O_BLOCKS - 1, passes(nt, w_codes, w_scales, ROW_ORDER))))
            final = result.tile([P, O_BLOCK, PLACES], F32)
            for h in ROW_ORDER:
                places = slice(h * SIDE, (h + 1) * SIDE)
                acc = passes(N_TILES - 1, w_codes, w_scales, (h,))[0][1]
                biased_row = rows.tile([P, O_BLOCK, SIDE], F32)
                nc.vector.tensor_tensor(
                    out=biased_row[:],
                    in0=acc[:].rearrange("p w o -> p o w"),
                    in1=bias_all[:, h, O_BLOCKS - 1, :, :],
                    op=ALU.add,
                )
                activated_row = rows.tile([P, O_BLOCK, SIDE], F32)
                nc.vector.scalar_tensor_tensor(
                    out=activated_row[:], in0=biased_row[:], scalar=NEG_SLOPE, in1=biased_row[:], op0=ALU.mult, op1=ALU.max
                )
                copy = nc.vector.tensor_copy if h == ROW_ORDER[-1] else nc.scalar.copy
                copy(out=final[:, :, places], in_=activated_row[:])
            store(O_BLOCKS - 1, N_TILES - 1, final)
